import numpy as np
import ml_dtypes


def mxq(x, axis, fmt="e4m3"):
    dtype, down = {"e4m3": (ml_dtypes.float8_e4m3fn, 7), "e5m2": (ml_dtypes.float8_e5m2, 14)}[fmt]
    v = np.moveaxis(np.asarray(x, np.float32).astype(ml_dtypes.bfloat16).astype(np.float64), axis, -1)
    blocks = v.reshape(v.shape[:-1] + (-1, 32))
    amax = np.abs(blocks).max(-1, keepdims=True)
    byte = np.maximum(np.where(amax > 0, np.frexp(amax)[1] - 1 + 127, 0) - down, 1)
    scale = np.exp2(byte - 127.0)
    codes = (blocks / scale).astype(np.float32).astype(dtype).astype(np.float64)
    return np.moveaxis((codes * scale).reshape(v.shape), -1, axis)


WIDE = False


def mx_kscale(k):
    if not WIDE:
        return np.ones(k)
    levels = np.array([10, -10, 5, -5, 0])
    a = np.random.permutation(np.resize(levels, k // 512 * 4)).reshape(k // 512, 4)
    idx = np.arange(k)
    return np.exp2(a[idx // 512, idx % 128 // 32])


BF16 = ml_dtypes.bfloat16


def bf(x):
    return np.asarray(x, np.float32).astype(BF16)


def f64(x):
    return np.asarray(x).astype(np.float64)


E2M1 = np.array([0.0, 0.5, 1.0, 1.5, 2.0, 3.0, 4.0, 6.0, -0.0, -0.5, -1.0, -1.5, -2.0, -3.0, -4.0, -6.0])


def pack_weight(w, fmt):
    k, n = w.shape
    w = f64(bf(w)).reshape(k // 32, 32, n)
    amax = np.abs(w).max(1)
    if fmt == "e4m3":
        byte = np.frexp(amax)[1] - 1 + 127 - 7
    else:
        mant, ex = np.frexp(amax / 6.0)
        byte = np.where(mant > 0.5, ex, ex - 1) + 127
    byte = np.clip(np.where(amax > 0, byte, 1), 1, 254)
    scaled = (w * np.exp2(127.0 - byte)[:, None, :]).reshape(k, n).astype(np.float32)
    by_word = np.ascontiguousarray(scaled.reshape(k // 512, 128, 4, n).transpose(0, 1, 3, 2))
    if fmt == "e4m3":
        words = by_word.astype(ml_dtypes.float8_e4m3fn).view(np.uint8)
    else:
        c = by_word.astype(ml_dtypes.float4_e2m1fn).view(np.uint8) & 0xF
        words = c[..., 0::2] | (c[..., 1::2] << 4)
    return np.ascontiguousarray(words), np.ascontiguousarray(byte.astype(np.uint8).reshape(k // 512, 16, n))


def unpack_weight(words, scales, fmt):
    g, p, n, _ = words.shape
    if fmt == "e4m3":
        vals = np.ascontiguousarray(words).view(ml_dtypes.float8_e4m3fn).astype(np.float64)
    else:
        nib = np.empty((g, p, n, 4), np.uint8)
        nib[..., 0::2] = words & 0xF
        nib[..., 1::2] = words >> 4
        vals = E2M1[nib]
    vals = vals * np.repeat(np.exp2(scales.astype(np.float64) - 127.0), 8, axis=1)[..., None]
    return vals.transpose(0, 1, 3, 2).reshape(g * 512, n)


B, S, H, NH, HD, TRAIN, NTK0, BASE = 1, 128, 8192, 16, 64, 8192, 4096, 10000
FMT = "e4m3"


def rotary_cos_sin(seq_len):
    eff = max(seq_len, TRAIN)
    scale = eff / TRAIN
    mscale = 1.0 if scale <= 1.0 else 0.1 * np.log(scale) + 1.0
    p = 1
    while p < 2 * eff / NTK0:
        p *= 2
    ntk_alpha = max(p - 1, 1)
    base = BASE * ntk_alpha ** (HD / (HD - 2))
    inv_freq = 1.0 / base ** (np.arange(0, HD, 2, dtype=np.float64) / HD)
    freqs = np.outer(np.arange(eff, dtype=np.float64), inv_freq)
    emb = np.concatenate([freqs, freqs], axis=-1)
    return (mscale * np.cos(emb))[:seq_len], (mscale * np.sin(emb))[:seq_len]


def rotate_half(x):
    x1, x2 = x[..., : HD // 2], x[..., HD // 2 :]
    return np.concatenate([-x2, x1], axis=-1)


def setup_inputs():
    s = mx_kscale(H)
    hidden_states = bf(np.random.standard_normal((B, S, H)) * s)
    wq = np.random.standard_normal((NH * HD, H)) / np.sqrt(H) / s
    wkv = np.random.standard_normal((2 * NH * HD, H)) / np.sqrt(H) / s
    Wq_words, Wq_scales = pack_weight(np.ascontiguousarray(wq.T), FMT)
    Wkv_words, Wkv_scales = pack_weight(np.ascontiguousarray(wkv.T), FMT)
    return {"hidden_states": hidden_states,
            "Wq_words": Wq_words, "Wq_scales": Wq_scales,
            "Wkv_words": Wkv_words, "Wkv_scales": Wkv_scales}


def reference(hidden_states, Wq_words, Wq_scales, Wkv_words, Wkv_scales):
    xq = mxq(f64(hidden_states), 2, "e4m3")
    q = (xq @ unpack_weight(Wq_words, Wq_scales, FMT)).reshape(B, S, NH, HD)
    kv = (xq @ unpack_weight(Wkv_words, Wkv_scales, FMT)).reshape(B, S, NH, 2 * HD)
    k, v = kv[..., :HD], kv[..., HD:]
    cos, sin = rotary_cos_sin(S)
    cos = cos[None, :, None, :]
    sin = sin[None, :, None, :]
    q_rot = q * cos + rotate_half(q) * sin
    k_rot = k * cos + rotate_half(k) * sin
    return q_rot, k_rot, v

@@ -1,0 +1,277 @@
+import math
+from contextlib import ExitStack
+
+import concourse.mybir as mybir
+from concourse.masks import make_identity
+
+F32 = mybir.dt.float32
+BF16 = mybir.dt.bfloat16
+I32 = mybir.dt.int32
+U32 = mybir.dt.uint32
+U8 = mybir.dt.uint8
+FP8X4 = mybir.dt.float8_e4m3fn_x4
+ALU = mybir.AluOpType
+ACT = mybir.ActivationFunctionType
+
+P = 128
+HIDDEN = 8192
+PACK = 4
+K_GROUP = P * PACK
+GROUPS = HIDDEN // K_GROUP
+HEADS = 16
+HEAD_DIM = 64
+HALF = HEAD_DIM // 2
+BANK_COLS = 512
+ROUND_BANKS = 2
+ROUND_COLS = ROUND_BANKS * BANK_COLS
+
+PLANES_PER_TILE = 4
+PLANE_SETS = GROUPS // PLANES_PER_TILE
+QUADRANTS = 4
+QUADRANT = 32
+SCALE_ROWS = 4
+
+X_PARTS = 4
+PART_GROUPS = GROUPS // X_PARTS
+WORDS_PER_GROUP = K_GROUP // 2
+
+WEIGHT_BUFS = 36
+
+ROPE_BASE = 10000.0 * 3.0 ** (HEAD_DIM / (HEAD_DIM - 2.0))
+FREQ_RATIO = ROPE_BASE ** (-1.0 / HALF)
+ROUND_MAGIC = 12582912.0
+TWO_PI_HIGH = 6.28125
+TWO_PI_LOW = 2.0 * math.pi - TWO_PI_HIGH
+
+FLOPS = 2 * P * HIDDEN * 3 * HEADS * HEAD_DIM
+
+
+def build_rotary_tables(nc, consts):
+    position_int = consts.tile([P, 1], I32)
+    nc.gpsimd.iota(position_int[:], pattern=[[0, 1]], base=0, channel_multiplier=1)
+    position = consts.tile([P, 1], F32)
+    nc.vector.tensor_copy(out=position[:], in_=position_int[:])
+
+    freq = consts.tile([P, HEAD_DIM], F32)
+    nc.vector.memset(freq[:, HALF : HALF + 1], 1.0)
+    for step in range(5):
+        width = 2**step
+        nc.vector.tensor_scalar(
+            out=freq[:, HALF + width : HALF + 2 * width],
+            in0=freq[:, HALF : HALF + width],
+            scalar1=FREQ_RATIO**width,
+            scalar2=None,
+            op0=ALU.mult,
+        )
+    nc.vector.tensor_scalar(
+        out=freq[:, 0:HALF], in0=freq[:, HALF:HEAD_DIM], scalar1=-1.0, scalar2=None, op0=ALU.mult
+    )
+    angle = consts.tile([P, HEAD_DIM], F32)
+    nc.vector.tensor_scalar(
+        out=angle[:], in0=freq[:], scalar1=position[:, 0:1], scalar2=None, op0=ALU.mult
+    )
+
+    turns = consts.tile([P, HEAD_DIM], F32)
+    nc.vector.tensor_scalar(
+        out=turns[:],
+        in0=angle[:],
+        scalar1=1.0 / (2.0 * math.pi),
+        scalar2=ROUND_MAGIC,
+        op0=ALU.mult,
+        op1=ALU.add,
+    )
+    whole_turns = consts.tile([P, HEAD_DIM], F32)
+    nc.vector.tensor_scalar(
+        out=whole_turns[:], in0=turns[:], scalar1=ROUND_MAGIC, scalar2=None, op0=ALU.subtract
+    )
+    nearly = consts.tile([P, HEAD_DIM], F32)
+    nc.vector.scalar_tensor_tensor(
+        out=nearly[:], in0=whole_turns[:], scalar=-TWO_PI_HIGH, in1=angle[:], op0=ALU.mult, op1=ALU.add
+    )
+    reduced = consts.tile([P, HEAD_DIM], F32)
+    nc.vector.scalar_tensor_tensor(
+        out=reduced[:], in0=whole_turns[:], scalar=-TWO_PI_LOW, in1=nearly[:], op0=ALU.mult, op1=ALU.add
+    )
+    minus_abs = consts.tile([P, HEAD_DIM], F32)
+    nc.vector.scalar_tensor_tensor(
+        out=minus_abs[:], in0=reduced[:], scalar=-1.0, in1=reduced[:], op0=ALU.mult, op1=ALU.min
+    )
+    shifted = consts.tile([P, HEAD_DIM], F32)
+    nc.vector.tensor_scalar(
+        out=shifted[:], in0=minus_abs[:], scalar1=math.pi / 2.0, scalar2=None, op0=ALU.add
+    )
+    sin_t = consts.tile([P, HEAD_DIM], F32)
+    nc.scalar.activation(out=sin_t[:], in_=reduced[:], func=ACT.Sin)
+    cos_t = consts.tile([P, HEAD_DIM], F32)
+    nc.scalar.activation(out=cos_t[:], in_=shifted[:], func=ACT.Sin)
+    return cos_t, sin_t
+
+
+def load_scale_planes(nc, planes, scales):
+    for s in range(PLANE_SETS):
+        for quadrant in range(QUADRANTS):
+            first = QUADRANT * quadrant
+            nc.sync.dma_start(
+                out=planes[first : first + PLANES_PER_TILE * SCALE_ROWS, s, :].bitcast(I32),
+                in_=scales[
+                    PLANES_PER_TILE * s : PLANES_PER_TILE * (s + 1),
+                    SCALE_ROWS * quadrant : SCALE_ROWS * (quadrant + 1),
+                    :,
+                ].bitcast(I32),
+            )
+
+
+def tile_telechatattention_pa_k_kernel(
+    tc, hidden_states, Wq_words, Wq_scales, Wkv_words, Wkv_scales, out_0, out_1, out_2
+):
+    nc = tc.nc
+    x = hidden_states.rearrange("b s k -> (b s) k")
+    q_words = Wq_words.rearrange("g p n t -> p g (n t)")
+    kv_words = Wkv_words.rearrange("g p n t -> p g (n t)")
+    q_rot = out_0.rearrange("b s h d -> (b s) h d")
+    k_rot = out_1.rearrange("b s h d -> (b s) h d")
+    v_out = out_2.rearrange("b s h d -> (b s) h d")
+
+    with ExitStack() as ctx:
+        ctx.enter_context(tc.manual_schedule())
+        consts = ctx.enter_context(tc.tile_pool(name="consts", bufs=1))
+        stage = ctx.enter_context(tc.tile_pool(name="stage", bufs=2))
+        weights = ctx.enter_context(tc.tile_pool(name="weights", bufs=WEIGHT_BUFS))
+        results = ctx.enter_context(tc.tile_pool(name="results", bufs=2))
+        psum_x = ctx.enter_context(tc.psum_pool(name="psum_x", bufs=4))
+        psum_acc = ctx.enter_context(tc.psum_pool(name="psum_acc", bufs=2 * ROUND_BANKS))
+
+        x_sb = consts.tile([P, HIDDEN], BF16)
+        part_cols = PART_GROUPS * K_GROUP
+        for part in range(X_PARTS):
+            cols = slice(part * part_cols, (part + 1) * part_cols)
+            nc.sync.dma_start(out=x_sb[:, cols], in_=x[:, cols])
+
+        q_planes = consts.tile([P, PLANE_SETS, ROUND_COLS], U8, align_bytes=64)
+        kv_planes = consts.tile([P, PLANE_SETS, 2 * ROUND_COLS], U8, align_bytes=64)
+        nc.vector.memset(q_planes[:].bitcast(I32), 0)
+        nc.vector.memset(kv_planes[:].bitcast(I32), 0)
+        load_scale_planes(nc, q_planes, Wq_scales)
+        load_scale_planes(nc, kv_planes, Wkv_scales)
+
+        cos_t, sin_t = build_rotary_tables(nc, consts)
+        identity = consts.tile([P, P], F32)
+        make_identity(nc, identity[:])
+
+        x_words = x_sb[:].bitcast(F32)
+        x_codes = consts.tile([P, GROUPS, P], U32, align_bytes=64)
+        x_scales = consts.tile([P, GROUPS, P], U8, align_bytes=64)
+        for part in range(X_PARTS):
+            grouped = stage.tile([P, PART_GROUPS, P, PACK], BF16, align_bytes=64)
+            grouped_words = grouped[:].bitcast(F32)
+            for pair in range(PART_GROUPS // 2):
+                turned = psum_x.tile([P, 2, 2, P], F32)
+                for i in range(2):
+                    first = (part * PART_GROUPS + 2 * pair + i) * WORDS_PER_GROUP
+                    for u in range(2):
+                        nc.tensor.transpose(
+                            out=turned[:, i, u, :],
+                            in_=x_words[:, first + u : first + WORDS_PER_GROUP : 2],
+                            identity=identity[:],
+                        )
+                copy = nc.vector.tensor_copy if pair == 0 else nc.scalar.copy
+                copy(
+                    out=grouped_words[:, 2 * pair : 2 * pair + 2, :, :],
+                    in_=turned[:].rearrange("p i u r -> p i r u"),
+                )
+            part_groups = slice(part * PART_GROUPS, (part + 1) * PART_GROUPS)
+            nc.vector.quantize_mx(
+                out=x_codes[:, part_groups, :].rearrange("p g r -> p (g r)").bitcast(FP8X4),
+                scales=x_scales[:, part_groups, :].rearrange("p g r -> p (g r)"),
+                in_=grouped[:].rearrange("p g r t -> p (g r t)"),
+            )
+
+        def project(words, planes, first_col):
+            banks = [
+                psum_acc.tile([P, BANK_COLS], F32, name="bank%d" % b, tag="bank")
+                for b in range(ROUND_BANKS)
+            ]
+            for g in range(GROUPS):
+                piece = weights.tile([P, ROUND_COLS], U32, align_bytes=64)
+                nc.sync.dma_start(
+                    out=piece[:].bitcast(I32),
+                    in_=words[:, g, PACK * first_col : PACK * (first_col + ROUND_COLS)].bitcast(I32),
+                )
+                s, j = divmod(g, PLANES_PER_TILE)
+                for b in range(ROUND_BANKS):
+                    nc.tensor.matmul_mx(
+                        out=banks[b][:],
+                        lhsT=x_codes[:, g, :].bitcast(FP8X4),
+                        lhsT_scale=x_scales[:, g, :],
+                        rhs=piece[:, b * BANK_COLS : (b + 1) * BANK_COLS].bitcast(FP8X4),
+                        rhs_scale=planes[
+                            SCALE_ROWS * j : P,
+                            s,
+                            first_col + b * BANK_COLS : first_col + (b + 1) * BANK_COLS,
+                        ],
+                        start=(g == 0),
+                        stop=(g == GROUPS - 1),
+                    )
+            return banks
+
+        def rotary_products(straight, crossed, heads):
+            n = heads.shape[1]
+            nc.vector.tensor_tensor(
+                out=straight,
+                in0=heads,
+                in1=cos_t[:].unsqueeze(1).to_broadcast([P, n, HEAD_DIM]),
+                op=ALU.mult,
+            )
+            nc.vector.tensor_tensor(
+                out=crossed[:, :, 0:HALF],
+                in0=heads[:, :, HALF:HEAD_DIM],
+                in1=sin_t[:, 0:HALF].unsqueeze(1).to_broadcast([P, n, HALF]),
+                op=ALU.mult,
+            )
+            nc.vector.tensor_tensor(
+                out=crossed[:, :, HALF:HEAD_DIM],
+                in0=heads[:, :, 0:HALF],
+                in1=sin_t[:, HALF:HEAD_DIM].unsqueeze(1).to_broadcast([P, n, HALF]),
+                op=ALU.mult,
+            )
+
+        banks = project(q_words, q_planes, 0)
+        straight = results.tile([P, HEADS, HEAD_DIM], F32, tag="straight")
+        crossed = results.tile([P, HEADS, HEAD_DIM], F32, tag="crossed")
+        bank_heads = BANK_COLS // HEAD_DIM
+        for b in range(ROUND_BANKS):
+            these = slice(b * bank_heads, (b + 1) * bank_heads)
+            rotary_products(
+                straight[:, these, :],
+                crossed[:, these, :],
+                banks[b][:].rearrange("p (h d) -> p h d", d=HEAD_DIM),
+            )
+        nc.vector.tensor_tensor(out=straight[:], in0=straight[:], in1=crossed[:], op=ALU.add)
+        nc.scalar.dma_start(out=q_rot, in_=straight[:])
+
+        bank_heads = BANK_COLS // (2 * HEAD_DIM)
+        round_heads = ROUND_BANKS * bank_heads
+        for half in range(2):
+            banks = project(kv_words, kv_planes, half * ROUND_COLS)
+            straight = results.tile([P, HEADS, HEAD_DIM], F32, tag="straight")
+            crossed = results.tile([P, HEADS, HEAD_DIM], F32, tag="crossed")
+            values = results.tile([P, round_heads, HEAD_DIM], F32, tag="values")
+            k_and_v = [
+                bank[:].rearrange("p (h c d) -> p h c d", c=2, d=HEAD_DIM) for bank in banks
+            ]
+            bank_slices = [slice(b * bank_heads, (b + 1) * bank_heads) for b in range(ROUND_BANKS)]
+            for b in range(ROUND_BANKS):
+                other = ROUND_BANKS - 1 - b
+                nc.scalar.copy(out=values[:, bank_slices[other], :], in_=k_and_v[other][:, :, 1, :])
+                rotary_products(
+                    straight[:, bank_slices[b], :], crossed[:, bank_slices[b], :], k_and_v[b][:, :, 0, :]
+                )
+            nc.vector.tensor_tensor(
+                out=straight[:, 0:round_heads, :],
+                in0=straight[:, 0:round_heads, :],
+                in1=crossed[:, 0:round_heads, :],
+                op=ALU.add,
+            )
+            out_heads = slice(half * round_heads, (half + 1) * round_heads)
+            nc.scalar.dma_start(out=v_out[:, out_heads, :], in_=values[:])
+            nc.scalar.dma_start(out=k_rot[:, out_heads, :], in_=straight[:, 0:round_heads, :])

@@ -121,6 +121,17 @@ def load_scale_planes(nc, planes, scales):
             )
 
 
+def trickle_scale_planes(nc, planes, scales):
+    by_row = scales.rearrange("(s j) q n -> q j s n", j=PLANES_PER_TILE)
+    for quadrant in range(QUADRANTS):
+        for r in range(SCALE_ROWS):
+            first = QUADRANT * quadrant + r
+            nc.gpsimd.dma_start(
+                out=planes[first : first + PLANES_PER_TILE * SCALE_ROWS : SCALE_ROWS, :, :].bitcast(F32),
+                in_=by_row[SCALE_ROWS * quadrant + r].bitcast(F32),
+            )
+
+
 def tile_telechatattention_pa_k_kernel(
     tc, hidden_states, Wq_words, Wq_scales, Wkv_words, Wkv_scales, out_0, out_1, out_2
 ):
@@ -152,11 +163,11 @@ def tile_telechatattention_pa_k_kernel(
         nc.vector.memset(q_planes[:].bitcast(I32), 0)
         nc.vector.memset(kv_planes[:].bitcast(I32), 0)
         load_scale_planes(nc, q_planes, Wq_scales)
-        load_scale_planes(nc, kv_planes, Wkv_scales)
 
         cos_t, sin_t = build_rotary_tables(nc, consts)
         identity = consts.tile([P, P], F32)
         make_identity(nc, identity[:])
+        trickle_scale_planes(nc, kv_planes, Wkv_scales)
 
         x_words = x_sb[:].bitcast(F32)
         x_codes = consts.tile([P, GROUPS, P], U32, align_bytes=64)

@@ -22,8 +22,11 @@ HEADS = 16
 HEAD_DIM = 64
 HALF = HEAD_DIM // 2
 BANK_COLS = 512
-ROUND_BANKS = 2
-ROUND_COLS = ROUND_BANKS * BANK_COLS
+Q_COLS = HEADS * HEAD_DIM
+KV_COLS = 2 * HEADS * HEAD_DIM
+Q_BANKS = Q_COLS // BANK_COLS
+KV_BANKS = KV_COLS // BANK_COLS
+TAIL_GROUPS = 2
 
 PLANES_PER_TILE = 4
 PLANE_SETS = GROUPS // PLANES_PER_TILE
@@ -35,7 +38,9 @@ X_PARTS = 4
 PART_GROUPS = GROUPS // X_PARTS
 WORDS_PER_GROUP = K_GROUP // 2
 
-WEIGHT_BUFS = 36
+Q_PIECE_BUFS = 12
+KV_PIECE_BUFS = 10
+TAIL_PIECE_BUFS = KV_BANKS * TAIL_GROUPS
 
 ROPE_BASE = 10000.0 * 3.0 ** (HEAD_DIM / (HEAD_DIM - 2.0))
 FREQ_RATIO = ROPE_BASE ** (-1.0 / HALF)
@@ -121,17 +126,6 @@ def load_scale_planes(nc, planes, scales):
             )
 
 
-def trickle_scale_planes(nc, planes, scales):
-    by_row = scales.rearrange("(s j) q n -> q j s n", j=PLANES_PER_TILE)
-    for quadrant in range(QUADRANTS):
-        for r in range(SCALE_ROWS):
-            first = QUADRANT * quadrant + r
-            nc.gpsimd.dma_start(
-                out=planes[first : first + PLANES_PER_TILE * SCALE_ROWS : SCALE_ROWS, :, :].bitcast(F32),
-                in_=by_row[SCALE_ROWS * quadrant + r].bitcast(F32),
-            )
-
-
 def tile_telechatattention_pa_k_kernel(
     tc, hidden_states, Wq_words, Wq_scales, Wkv_words, Wkv_scales, out_0, out_1, out_2
 ):
@@ -147,27 +141,26 @@ def tile_telechatattention_pa_k_kernel(
         ctx.enter_context(tc.manual_schedule())
         consts = ctx.enter_context(tc.tile_pool(name="consts", bufs=1))
         stage = ctx.enter_context(tc.tile_pool(name="stage", bufs=2))
-        weights = ctx.enter_context(tc.tile_pool(name="weights", bufs=WEIGHT_BUFS))
-        results = ctx.enter_context(tc.tile_pool(name="results", bufs=2))
-        psum_x = ctx.enter_context(tc.psum_pool(name="psum_x", bufs=4))
-        psum_acc = ctx.enter_context(tc.psum_pool(name="psum_acc", bufs=2 * ROUND_BANKS))
+        q_pieces = ctx.enter_context(tc.tile_pool(name="q_pieces", bufs=Q_PIECE_BUFS))
+        kv_pieces = ctx.enter_context(tc.tile_pool(name="kv_pieces", bufs=KV_PIECE_BUFS))
+        tail_pieces = ctx.enter_context(tc.tile_pool(name="tail_pieces", bufs=TAIL_PIECE_BUFS))
+        kv_results = ctx.enter_context(tc.tile_pool(name="kv_results", bufs=KV_BANKS))
+        psum_x = ctx.enter_context(tc.psum_pool(name="psum_x", bufs=2))
+        psum_out = ctx.enter_context(tc.psum_pool(name="psum_out", bufs=1))
 
         x_sb = consts.tile([P, HIDDEN], BF16)
-        part_cols = PART_GROUPS * K_GROUP
-        for part in range(X_PARTS):
-            cols = slice(part * part_cols, (part + 1) * part_cols)
-            nc.sync.dma_start(out=x_sb[:, cols], in_=x[:, cols])
+        nc.sync.dma_start(out=x_sb[:], in_=x)
 
-        q_planes = consts.tile([P, PLANE_SETS, ROUND_COLS], U8, align_bytes=64)
-        kv_planes = consts.tile([P, PLANE_SETS, 2 * ROUND_COLS], U8, align_bytes=64)
+        q_planes = consts.tile([P, PLANE_SETS, Q_COLS], U8, align_bytes=64)
+        kv_planes = consts.tile([P, PLANE_SETS, KV_COLS], U8, align_bytes=64)
         nc.vector.memset(q_planes[:].bitcast(I32), 0)
         nc.vector.memset(kv_planes[:].bitcast(I32), 0)
         load_scale_planes(nc, q_planes, Wq_scales)
+        load_scale_planes(nc, kv_planes, Wkv_scales)
 
         cos_t, sin_t = build_rotary_tables(nc, consts)
         identity = consts.tile([P, P], F32)
         make_identity(nc, identity[:])
-        trickle_scale_planes(nc, kv_planes, Wkv_scales)
 
         x_words = x_sb[:].bitcast(F32)
         x_codes = consts.tile([P, GROUPS, P], U32, align_bytes=64)
@@ -197,21 +190,18 @@ def tile_telechatattention_pa_k_kernel(
                 in_=grouped[:].rearrange("p g r t -> p (g r t)"),
             )
 
-        def project(words, planes, first_col):
-            banks = [
-                psum_acc.tile([P, BANK_COLS], F32, name="bank%d" % b, tag="bank")
-                for b in range(ROUND_BANKS)
-            ]
-            for g in range(GROUPS):
-                piece = weights.tile([P, ROUND_COLS], U32, align_bytes=64)
+        def accumulate(pieces, words, planes, banks, first_col, groups):
+            width = len(banks) * BANK_COLS
+            for g in groups:
+                piece = pieces.tile([P, width], U32, align_bytes=64)
                 nc.sync.dma_start(
                     out=piece[:].bitcast(I32),
-                    in_=words[:, g, PACK * first_col : PACK * (first_col + ROUND_COLS)].bitcast(I32),
+                    in_=words[:, g, PACK * first_col : PACK * (first_col + width)].bitcast(I32),
                 )
                 s, j = divmod(g, PLANES_PER_TILE)
-                for b in range(ROUND_BANKS):
+                for b, bank in enumerate(banks):
                     nc.tensor.matmul_mx(
-                        out=banks[b][:],
+                        out=bank[:],
                         lhsT=x_codes[:, g, :].bitcast(FP8X4),
                         lhsT_scale=x_scales[:, g, :],
                         rhs=piece[:, b * BANK_COLS : (b + 1) * BANK_COLS].bitcast(FP8X4),
@@ -223,12 +213,11 @@ def tile_telechatattention_pa_k_kernel(
                         start=(g == 0),
                         stop=(g == GROUPS - 1),
                     )
-            return banks
 
-        def rotary_products(straight, crossed, heads):
+        def rotate(rotated, crossed, heads):
             n = heads.shape[1]
             nc.vector.tensor_tensor(
-                out=straight,
+                out=rotated,
                 in0=heads,
                 in1=cos_t[:].unsqueeze(1).to_broadcast([P, n, HEAD_DIM]),
                 op=ALU.mult,
@@ -245,44 +234,42 @@ def tile_telechatattention_pa_k_kernel(
                 in1=sin_t[:, HALF:HEAD_DIM].unsqueeze(1).to_broadcast([P, n, HALF]),
                 op=ALU.mult,
             )
+            nc.vector.tensor_tensor(out=rotated, in0=rotated, in1=crossed, op=ALU.add)
 
-        banks = project(q_words, q_planes, 0)
-        straight = results.tile([P, HEADS, HEAD_DIM], F32, tag="straight")
-        crossed = results.tile([P, HEADS, HEAD_DIM], F32, tag="crossed")
-        bank_heads = BANK_COLS // HEAD_DIM
-        for b in range(ROUND_BANKS):
-            these = slice(b * bank_heads, (b + 1) * bank_heads)
-            rotary_products(
-                straight[:, these, :],
-                crossed[:, these, :],
-                banks[b][:].rearrange("p (h d) -> p h d", d=HEAD_DIM),
+        q_banks = [psum_out.tile([P, BANK_COLS], F32, name="q_bank%d" % b) for b in range(Q_BANKS)]
+        accumulate(q_pieces, q_words, q_planes, q_banks, 0, range(GROUPS))
+        q_rotated = consts.tile([P, HEADS, HEAD_DIM], F32)
+        q_crossed = consts.tile([P, HEADS, HEAD_DIM], F32)
+        q_bank_heads = BANK_COLS // HEAD_DIM
+        for b in range(Q_BANKS):
+            these = slice(b * q_bank_heads, (b + 1) * q_bank_heads)
+            rotate(
+                q_rotated[:, these, :],
+                q_crossed[:, these, :],
+                q_banks[b][:].rearrange("p (h d) -> p h d", d=HEAD_DIM),
             )
-        nc.vector.tensor_tensor(out=straight[:], in0=straight[:], in1=crossed[:], op=ALU.add)
-        nc.scalar.dma_start(out=q_rot, in_=straight[:])
 
-        bank_heads = BANK_COLS // (2 * HEAD_DIM)
-        round_heads = ROUND_BANKS * bank_heads
-        for half in range(2):
-            banks = project(kv_words, kv_planes, half * ROUND_COLS)
-            straight = results.tile([P, HEADS, HEAD_DIM], F32, tag="straight")
-            crossed = results.tile([P, HEADS, HEAD_DIM], F32, tag="crossed")
-            values = results.tile([P, round_heads, HEAD_DIM], F32, tag="values")
-            k_and_v = [
-                bank[:].rearrange("p (h c d) -> p h c d", c=2, d=HEAD_DIM) for bank in banks
-            ]
-            bank_slices = [slice(b * bank_heads, (b + 1) * bank_heads) for b in range(ROUND_BANKS)]
-            for b in range(ROUND_BANKS):
-                other = ROUND_BANKS - 1 - b
-                nc.scalar.copy(out=values[:, bank_slices[other], :], in_=k_and_v[other][:, :, 1, :])
-                rotary_products(
-                    straight[:, bank_slices[b], :], crossed[:, bank_slices[b], :], k_and_v[b][:, :, 0, :]
-                )
-            nc.vector.tensor_tensor(
-                out=straight[:, 0:round_heads, :],
-                in0=straight[:, 0:round_heads, :],
-                in1=crossed[:, 0:round_heads, :],
-                op=ALU.add,
+        kv_banks = [psum_out.tile([P, BANK_COLS], F32, name="kv_bank%d" % b) for b in range(KV_BANKS)]
+        accumulate(kv_pieces, kv_words, kv_planes, kv_banks, 0, range(GROUPS - TAIL_GROUPS))
+        for b in range(KV_BANKS):
+            accumulate(
+                tail_pieces,
+                kv_words,
+                kv_planes,
+                kv_banks[b : b + 1],
+                b * BANK_COLS,
+                range(GROUPS - TAIL_GROUPS, GROUPS),
             )
-            out_heads = slice(half * round_heads, (half + 1) * round_heads)
-            nc.scalar.dma_start(out=v_out[:, out_heads, :], in_=values[:])
-            nc.scalar.dma_start(out=k_rot[:, out_heads, :], in_=straight[:, 0:round_heads, :])
+
+        nc.sync.dma_start(out=q_rot, in_=q_rotated[:])
+        kv_bank_heads = BANK_COLS // (2 * HEAD_DIM)
+        for b in range(KV_BANKS):
+            these = slice(b * kv_bank_heads, (b + 1) * kv_bank_heads)
+            k_and_v = kv_banks[b][:].rearrange("p (h c d) -> p h c d", c=2, d=HEAD_DIM)
+            k_rotated = kv_results.tile([P, kv_bank_heads, HEAD_DIM], F32)
+            k_crossed = kv_results.tile([P, kv_bank_heads, HEAD_DIM], F32)
+            values = kv_results.tile([P, kv_bank_heads, HEAD_DIM], F32)
+            rotate(k_rotated[:], k_crossed[:], k_and_v[:, :, 0, :])
+            nc.scalar.copy(out=values[:], in_=k_and_v[:, :, 1, :])
+            nc.sync.dma_start(out=k_rot[:, these, :], in_=k_rotated[:])
+            nc.sync.dma_start(out=v_out[:, these, :], in_=values[:])

@@ -112,9 +112,10 @@ def build_rotary_tables(nc, consts):
     return cos_t, sin_t
 
 
-def load_scale_planes(nc, planes, scales):
-    for s in range(PLANE_SETS):
-        for quadrant in range(QUADRANTS):
+def load_scale_set(nc, planes, scales, s):
+    for low in range(QUADRANTS // 2):
+        for half in range(2):
+            quadrant = (QUADRANTS // 2) * half + low
             first = QUADRANT * quadrant
             nc.sync.dma_start(
                 out=planes[first : first + PLANES_PER_TILE * SCALE_ROWS, s, :].bitcast(I32),
@@ -155,8 +156,6 @@ def tile_telechatattention_pa_k_kernel(
         kv_planes = consts.tile([P, PLANE_SETS, KV_COLS], U8, align_bytes=64)
         nc.vector.memset(q_planes[:].bitcast(I32), 0)
         nc.vector.memset(kv_planes[:].bitcast(I32), 0)
-        load_scale_planes(nc, q_planes, Wq_scales)
-        load_scale_planes(nc, kv_planes, Wkv_scales)
 
         cos_t, sin_t = build_rotary_tables(nc, consts)
         identity = consts.tile([P, P], F32)
@@ -190,15 +189,18 @@ def tile_telechatattention_pa_k_kernel(
                 in_=grouped[:].rearrange("p g r t -> p (g r t)"),
             )
 
-        def accumulate(pieces, words, planes, banks, first_col, groups):
+        def accumulate(pieces, weight, banks, first_col, groups):
+            words, scales, planes = weight
             width = len(banks) * BANK_COLS
             for g in groups:
+                s, j = divmod(g, PLANES_PER_TILE)
+                if j == 0:
+                    load_scale_set(nc, planes, scales, s)
                 piece = pieces.tile([P, width], U32, align_bytes=64)
                 nc.sync.dma_start(
                     out=piece[:].bitcast(I32),
                     in_=words[:, g, PACK * first_col : PACK * (first_col + width)].bitcast(I32),
                 )
-                s, j = divmod(g, PLANES_PER_TILE)
                 for b, bank in enumerate(banks):
                     nc.tensor.matmul_mx(
                         out=bank[:],
@@ -237,7 +239,7 @@ def tile_telechatattention_pa_k_kernel(
             nc.vector.tensor_tensor(out=rotated, in0=rotated, in1=crossed, op=ALU.add)
 
         q_banks = [psum_out.tile([P, BANK_COLS], F32, name="q_bank%d" % b) for b in range(Q_BANKS)]
-        accumulate(q_pieces, q_words, q_planes, q_banks, 0, range(GROUPS))
+        accumulate(q_pieces, (q_words, Wq_scales, q_planes), q_banks, 0, range(GROUPS))
         q_rotated = consts.tile([P, HEADS, HEAD_DIM], F32)
         q_crossed = consts.tile([P, HEADS, HEAD_DIM], F32)
         q_bank_heads = BANK_COLS // HEAD_DIM
@@ -250,12 +252,12 @@ def tile_telechatattention_pa_k_kernel(
             )
 
         kv_banks = [psum_out.tile([P, BANK_COLS], F32, name="kv_bank%d" % b) for b in range(KV_BANKS)]
-        accumulate(kv_pieces, kv_words, kv_planes, kv_banks, 0, range(GROUPS - TAIL_GROUPS))
+        kv_weight = (kv_words, Wkv_scales, kv_planes)
+        accumulate(kv_pieces, kv_weight, kv_banks, 0, range(GROUPS - TAIL_GROUPS))
         for b in range(KV_BANKS):
             accumulate(
                 tail_pieces,
-                kv_words,
-                kv_planes,
+                kv_weight,
                 kv_banks[b : b + 1],
                 b * BANK_COLS,
                 range(GROUPS - TAIL_GROUPS, GROUPS),
@@ -271,5 +273,5 @@ def tile_telechatattention_pa_k_kernel(
             values = kv_results.tile([P, kv_bank_heads, HEAD_DIM], F32)
             rotate(k_rotated[:], k_crossed[:], k_and_v[:, :, 0, :])
             nc.scalar.copy(out=values[:], in_=k_and_v[:, :, 1, :])
-            nc.sync.dma_start(out=k_rot[:, these, :], in_=k_rotated[:])
             nc.sync.dma_start(out=v_out[:, these, :], in_=values[:])
+            nc.sync.dma_start(out=k_rot[:, these, :], in_=k_rotated[:])

@@ -112,19 +112,20 @@ def build_rotary_tables(nc, consts):
     return cos_t, sin_t
 
 
-def load_scale_set(nc, planes, scales, s):
-    for low in range(QUADRANTS // 2):
-        for half in range(2):
-            quadrant = (QUADRANTS // 2) * half + low
-            first = QUADRANT * quadrant
-            nc.sync.dma_start(
-                out=planes[first : first + PLANES_PER_TILE * SCALE_ROWS, s, :].bitcast(I32),
-                in_=scales[
-                    PLANES_PER_TILE * s : PLANES_PER_TILE * (s + 1),
-                    SCALE_ROWS * quadrant : SCALE_ROWS * (quadrant + 1),
-                    :,
-                ].bitcast(I32),
-            )
+def load_scale_planes(nc, planes, scales):
+    for s in range(PLANE_SETS):
+        for low in range(QUADRANTS // 2):
+            for half in range(2):
+                quadrant = (QUADRANTS // 2) * half + low
+                first = QUADRANT * quadrant
+                nc.sync.dma_start(
+                    out=planes[first : first + PLANES_PER_TILE * SCALE_ROWS, s, :].bitcast(I32),
+                    in_=scales[
+                        PLANES_PER_TILE * s : PLANES_PER_TILE * (s + 1),
+                        SCALE_ROWS * quadrant : SCALE_ROWS * (quadrant + 1),
+                        :,
+                    ].bitcast(I32),
+                )
 
 
 def tile_telechatattention_pa_k_kernel(
@@ -156,6 +157,8 @@ def tile_telechatattention_pa_k_kernel(
         kv_planes = consts.tile([P, PLANE_SETS, KV_COLS], U8, align_bytes=64)
         nc.vector.memset(q_planes[:].bitcast(I32), 0)
         nc.vector.memset(kv_planes[:].bitcast(I32), 0)
+        load_scale_planes(nc, q_planes, Wq_scales)
+        load_scale_planes(nc, kv_planes, Wkv_scales)
 
         cos_t, sin_t = build_rotary_tables(nc, consts)
         identity = consts.tile([P, P], F32)
@@ -189,18 +192,15 @@ def tile_telechatattention_pa_k_kernel(
                 in_=grouped[:].rearrange("p g r t -> p (g r t)"),
             )
 
-        def accumulate(pieces, weight, banks, first_col, groups):
-            words, scales, planes = weight
+        def accumulate(pieces, words, planes, banks, first_col, groups):
             width = len(banks) * BANK_COLS
             for g in groups:
-                s, j = divmod(g, PLANES_PER_TILE)
-                if j == 0:
-                    load_scale_set(nc, planes, scales, s)
                 piece = pieces.tile([P, width], U32, align_bytes=64)
                 nc.sync.dma_start(
                     out=piece[:].bitcast(I32),
                     in_=words[:, g, PACK * first_col : PACK * (first_col + width)].bitcast(I32),
                 )
+                s, j = divmod(g, PLANES_PER_TILE)
                 for b, bank in enumerate(banks):
                     nc.tensor.matmul_mx(
                         out=bank[:],
@@ -239,7 +239,7 @@ def tile_telechatattention_pa_k_kernel(
             nc.vector.tensor_tensor(out=rotated, in0=rotated, in1=crossed, op=ALU.add)
 
         q_banks = [psum_out.tile([P, BANK_COLS], F32, name="q_bank%d" % b) for b in range(Q_BANKS)]
-        accumulate(q_pieces, (q_words, Wq_scales, q_planes), q_banks, 0, range(GROUPS))
+        accumulate(q_pieces, q_words, q_planes, q_banks, 0, range(GROUPS))
         q_rotated = consts.tile([P, HEADS, HEAD_DIM], F32)
         q_crossed = consts.tile([P, HEADS, HEAD_DIM], F32)
         q_bank_heads = BANK_COLS // HEAD_DIM
@@ -252,12 +252,12 @@ def tile_telechatattention_pa_k_kernel(
             )
 
         kv_banks = [psum_out.tile([P, BANK_COLS], F32, name="kv_bank%d" % b) for b in range(KV_BANKS)]
-        kv_weight = (kv_words, Wkv_scales, kv_planes)
-        accumulate(kv_pieces, kv_weight, kv_banks, 0, range(GROUPS - TAIL_GROUPS))
+        accumulate(kv_pieces, kv_words, kv_planes, kv_banks, 0, range(GROUPS - TAIL_GROUPS))
         for b in range(KV_BANKS):
             accumulate(
                 tail_pieces,
-                kv_weight,
+                kv_words,
+                kv_planes,
                 kv_banks[b : b + 1],
                 b * BANK_COLS,
                 range(GROUPS - TAIL_GROUPS, GROUPS),
@@ -273,5 +273,5 @@ def tile_telechatattention_pa_k_kernel(
             values = kv_results.tile([P, kv_bank_heads, HEAD_DIM], F32)
             rotate(k_rotated[:], k_crossed[:], k_and_v[:, :, 0, :])
             nc.scalar.copy(out=values[:], in_=k_and_v[:, :, 1, :])
-            nc.sync.dma_start(out=v_out[:, these, :], in_=values[:])
             nc.sync.dma_start(out=k_rot[:, these, :], in_=k_rotated[:])
+            nc.sync.dma_start(out=v_out[:, these, :], in_=values[:])

@@ -26,7 +26,7 @@ Q_COLS = HEADS * HEAD_DIM
 KV_COLS = 2 * HEADS * HEAD_DIM
 Q_BANKS = Q_COLS // BANK_COLS
 KV_BANKS = KV_COLS // BANK_COLS
-TAIL_GROUPS = 2
+TAIL_GROUPS = 3
 
 PLANES_PER_TILE = 4
 PLANE_SETS = GROUPS // PLANES_PER_TILE
@@ -39,7 +39,7 @@ PART_GROUPS = GROUPS // X_PARTS
 WORDS_PER_GROUP = K_GROUP // 2
 
 Q_PIECE_BUFS = 12
-KV_PIECE_BUFS = 10
+KV_PIECE_BUFS = 9
 TAIL_PIECE_BUFS = KV_BANKS * TAIL_GROUPS
 
 ROPE_BASE = 10000.0 * 3.0 ** (HEAD_DIM / (HEAD_DIM - 2.0))
@@ -225,15 +225,12 @@ def tile_telechatattention_pa_k_kernel(
                 op=ALU.mult,
             )
             nc.vector.tensor_tensor(
-                out=crossed[:, :, 0:HALF],
-                in0=heads[:, :, HALF:HEAD_DIM],
-                in1=sin_t[:, 0:HALF].unsqueeze(1).to_broadcast([P, n, HALF]),
-                op=ALU.mult,
-            )
-            nc.vector.tensor_tensor(
-                out=crossed[:, :, HALF:HEAD_DIM],
-                in0=heads[:, :, 0:HALF],
-                in1=sin_t[:, HALF:HEAD_DIM].unsqueeze(1).to_broadcast([P, n, HALF]),
+                out=crossed.rearrange("p h (two d) -> p h two d", two=2),
+                in0=heads.rearrange("p h (two d) -> p h two d", two=2)[:, :, ::-1, :],
+                in1=sin_t[:]
+                .rearrange("p (two d) -> p two d", two=2)
+                .unsqueeze(1)
+                .to_broadcast([P, n, 2, HALF]),
                 op=ALU.mult,
             )
             nc.vector.tensor_tensor(out=rotated, in0=rotated, in1=crossed, op=ALU.add)

@@ -26,7 +26,7 @@ Q_COLS = HEADS * HEAD_DIM
 KV_COLS = 2 * HEADS * HEAD_DIM
 Q_BANKS = Q_COLS // BANK_COLS
 KV_BANKS = KV_COLS // BANK_COLS
-TAIL_GROUPS = 3
+TAIL_GROUPS = 4
 
 PLANES_PER_TILE = 4
 PLANE_SETS = GROUPS // PLANES_PER_TILE
@@ -39,8 +39,8 @@ PART_GROUPS = GROUPS // X_PARTS
 WORDS_PER_GROUP = K_GROUP // 2
 
 Q_PIECE_BUFS = 12
-KV_PIECE_BUFS = 9
-TAIL_PIECE_BUFS = KV_BANKS * TAIL_GROUPS
+KV_PIECE_BUFS = 10
+TAIL_PIECE_BUFS = 1
 
 ROPE_BASE = 10000.0 * 3.0 ** (HEAD_DIM / (HEAD_DIM - 2.0))
 FREQ_RATIO = ROPE_BASE ** (-1.0 / HALF)
@@ -249,26 +249,52 @@ def tile_telechatattention_pa_k_kernel(
             )
 
         kv_banks = [psum_out.tile([P, BANK_COLS], F32, name="kv_bank%d" % b) for b in range(KV_BANKS)]
-        accumulate(kv_pieces, kv_words, kv_planes, kv_banks, 0, range(GROUPS - TAIL_GROUPS))
-        for b in range(KV_BANKS):
-            accumulate(
-                tail_pieces,
-                kv_words,
-                kv_planes,
-                kv_banks[b : b + 1],
-                b * BANK_COLS,
-                range(GROUPS - TAIL_GROUPS, GROUPS),
+        whole = GROUPS - TAIL_GROUPS
+        accumulate(kv_pieces, kv_words, kv_planes, kv_banks, 0, range(whole))
+        stairs = [
+            (whole + 2, 0, 3),
+            (whole + 3, 0, 3),
+            (whole + 1, 0, 2),
+            (whole, 0, 1),
+            (whole, 1, 3),
+            (whole + 1, 2, 2),
+            (whole + 2, 3, 1),
+            (whole + 3, 3, 1),
+        ]
+        passes_done = [whole] * KV_BANKS
+        for step, (g, first_bank, n_banks) in enumerate(stairs):
+            piece = tail_pieces.tile([P, n_banks * BANK_COLS], U32, align_bytes=64, name="stair%d" % step)
+            first_col = first_bank * BANK_COLS
+            nc.sync.dma_start(
+                out=piece[:].bitcast(I32),
+                in_=kv_words[:, g, PACK * first_col : PACK * (first_col + n_banks * BANK_COLS)].bitcast(I32),
             )
+            s, j = divmod(g, PLANES_PER_TILE)
+            for i in range(n_banks):
+                b = first_bank + i
+                passes_done[b] += 1
+                nc.tensor.matmul_mx(
+                    out=kv_banks[b][:],
+                    lhsT=x_codes[:, g, :].bitcast(FP8X4),
+                    lhsT_scale=x_scales[:, g, :],
+                    rhs=piece[:, i * BANK_COLS : (i + 1) * BANK_COLS].bitcast(FP8X4),
+                    rhs_scale=kv_planes[SCALE_ROWS * j : P, s, b * BANK_COLS : (b + 1) * BANK_COLS],
+                    start=False,
+                    stop=(passes_done[b] == GROUPS),
+                )
 
         nc.sync.dma_start(out=q_rot, in_=q_rotated[:])
         kv_bank_heads = BANK_COLS // (2 * HEAD_DIM)
+        k_rotated = consts.tile([P, HEADS, HEAD_DIM], F32)
+        values = consts.tile([P, HEADS, HEAD_DIM], F32)
+        stored_after = {1: 0, 2: 2, 3: 3}
         for b in range(KV_BANKS):
             these = slice(b * kv_bank_heads, (b + 1) * kv_bank_heads)
             k_and_v = kv_banks[b][:].rearrange("p (h c d) -> p h c d", c=2, d=HEAD_DIM)
-            k_rotated = kv_results.tile([P, kv_bank_heads, HEAD_DIM], F32)
             k_crossed = kv_results.tile([P, kv_bank_heads, HEAD_DIM], F32)
-            values = kv_results.tile([P, kv_bank_heads, HEAD_DIM], F32)
-            rotate(k_rotated[:], k_crossed[:], k_and_v[:, :, 0, :])
-            nc.scalar.copy(out=values[:], in_=k_and_v[:, :, 1, :])
-            nc.sync.dma_start(out=k_rot[:, these, :], in_=k_rotated[:])
-            nc.sync.dma_start(out=v_out[:, these, :], in_=values[:])
+            rotate(k_rotated[:, these, :], k_crossed[:], k_and_v[:, :, 0, :])
+            nc.scalar.copy(out=values[:, these, :], in_=k_and_v[:, :, 1, :])
+            if b in stored_after:
+                ready = slice(stored_after[b] * kv_bank_heads, (b + 1) * kv_bank_heads)
+                nc.sync.dma_start(out=k_rot[:, ready, :], in_=k_rotated[:, ready, :])
+                nc.sync.dma_start(out=v_out[:, ready, :], in_=values[:, ready, :])

@@ -296,5 +296,5 @@ def tile_telechatattention_pa_k_kernel(
             nc.scalar.copy(out=values[:, these, :], in_=k_and_v[:, :, 1, :])
             if b in stored_after:
                 ready = slice(stored_after[b] * kv_bank_heads, (b + 1) * kv_bank_heads)
-                nc.sync.dma_start(out=k_rot[:, ready, :], in_=k_rotated[:, ready, :])
                 nc.sync.dma_start(out=v_out[:, ready, :], in_=values[:, ready, :])
+                nc.sync.dma_start(out=k_rot[:, ready, :], in_=k_rotated[:, ready, :])

import math
from contextlib import ExitStack

import concourse.mybir as mybir
from concourse.masks import make_identity

F32 = mybir.dt.float32
BF16 = mybir.dt.bfloat16
I32 = mybir.dt.int32
U32 = mybir.dt.uint32
U8 = mybir.dt.uint8
FP8X4 = mybir.dt.float8_e4m3fn_x4
ALU = mybir.AluOpType
ACT = mybir.ActivationFunctionType

P = 128
HIDDEN = 8192
PACK = 4
K_GROUP = P * PACK
GROUPS = HIDDEN // K_GROUP
HEADS = 16
HEAD_DIM = 64
HALF = HEAD_DIM // 2
BANK_COLS = 512
Q_COLS = HEADS * HEAD_DIM
KV_COLS = 2 * HEADS * HEAD_DIM
Q_BANKS = Q_COLS // BANK_COLS
KV_BANKS = KV_COLS // BANK_COLS
TAIL_GROUPS = 4

PLANES_PER_TILE = 4
PLANE_SETS = GROUPS // PLANES_PER_TILE
QUADRANTS = 4
QUADRANT = 32
SCALE_ROWS = 4

X_PARTS = 4
PART_GROUPS = GROUPS // X_PARTS
WORDS_PER_GROUP = K_GROUP // 2

Q_PIECE_BUFS = 12
KV_PIECE_BUFS = 10
TAIL_PIECE_BUFS = 1

ROPE_BASE = 10000.0 * 3.0 ** (HEAD_DIM / (HEAD_DIM - 2.0))
FREQ_RATIO = ROPE_BASE ** (-1.0 / HALF)
ROUND_MAGIC = 12582912.0
TWO_PI_HIGH = 6.28125
TWO_PI_LOW = 2.0 * math.pi - TWO_PI_HIGH

FLOPS = 2 * P * HIDDEN * 3 * HEADS * HEAD_DIM


def build_rotary_tables(nc, consts):
    position_int = consts.tile([P, 1], I32)
    nc.gpsimd.iota(position_int[:], pattern=[[0, 1]], base=0, channel_multiplier=1)
    position = consts.tile([P, 1], F32)
    nc.vector.tensor_copy(out=position[:], in_=position_int[:])

    freq = consts.tile([P, HEAD_DIM], F32)
    nc.vector.memset(freq[:, HALF : HALF + 1], 1.0)
    for step in range(5):
        width = 2**step
        nc.vector.tensor_scalar(
            out=freq[:, HALF + width : HALF + 2 * width],
            in0=freq[:, HALF : HALF + width],
            scalar1=FREQ_RATIO**width,
            scalar2=None,
            op0=ALU.mult,
        )
    nc.vector.tensor_scalar(
        out=freq[:, 0:HALF], in0=freq[:, HALF:HEAD_DIM], scalar1=-1.0, scalar2=None, op0=ALU.mult
    )
    angle = consts.tile([P, HEAD_DIM], F32)
    nc.vector.tensor_scalar(
        out=angle[:], in0=freq[:], scalar1=position[:, 0:1], scalar2=None, op0=ALU.mult
    )

    turns = consts.tile([P, HEAD_DIM], F32)
    nc.vector.tensor_scalar(
        out=turns[:],
        in0=angle[:],
        scalar1=1.0 / (2.0 * math.pi),
        scalar2=ROUND_MAGIC,
        op0=ALU.mult,
        op1=ALU.add,
    )
    whole_turns = consts.tile([P, HEAD_DIM], F32)
    nc.vector.tensor_scalar(
        out=whole_turns[:], in0=turns[:], scalar1=ROUND_MAGIC, scalar2=None, op0=ALU.subtract
    )
    nearly = consts.tile([P, HEAD_DIM], F32)
    nc.vector.scalar_tensor_tensor(
        out=nearly[:], in0=whole_turns[:], scalar=-TWO_PI_HIGH, in1=angle[:], op0=ALU.mult, op1=ALU.add
    )
    reduced = consts.tile([P, HEAD_DIM], F32)
    nc.vector.scalar_tensor_tensor(
        out=reduced[:], in0=whole_turns[:], scalar=-TWO_PI_LOW, in1=nearly[:], op0=ALU.mult, op1=ALU.add
    )
    minus_abs = consts.tile([P, HEAD_DIM], F32)
    nc.vector.scalar_tensor_tensor(
        out=minus_abs[:], in0=reduced[:], scalar=-1.0, in1=reduced[:], op0=ALU.mult, op1=ALU.min
    )
    shifted = consts.tile([P, HEAD_DIM], F32)
    nc.vector.tensor_scalar(
        out=shifted[:], in0=minus_abs[:], scalar1=math.pi / 2.0, scalar2=None, op0=ALU.add
    )
    sin_t = consts.tile([P, HEAD_DIM], F32)
    nc.scalar.activation(out=sin_t[:], in_=reduced[:], func=ACT.Sin)
    cos_t = consts.tile([P, HEAD_DIM], F32)
    nc.scalar.activation(out=cos_t[:], in_=shifted[:], func=ACT.Sin)
    return cos_t, sin_t


def load_scale_planes(nc, planes, scales):
    for s in range(PLANE_SETS):
        for low in range(QUADRANTS // 2):
            for half in range(2):
                quadrant = (QUADRANTS // 2) * half + low
                first = QUADRANT * quadrant
                nc.sync.dma_start(
                    out=planes[first : first + PLANES_PER_TILE * SCALE_ROWS, s, :].bitcast(I32),
                    in_=scales[
                        PLANES_PER_TILE * s : PLANES_PER_TILE * (s + 1),
                        SCALE_ROWS * quadrant : SCALE_ROWS * (quadrant + 1),
                        :,
                    ].bitcast(I32),
                )


def tile_telechatattention_pa_k_kernel(
    tc, hidden_states, Wq_words, Wq_scales, Wkv_words, Wkv_scales, out_0, out_1, out_2
):
    nc = tc.nc
    x = hidden_states.rearrange("b s k -> (b s) k")
    q_words = Wq_words.rearrange("g p n t -> p g (n t)")
    kv_words = Wkv_words.rearrange("g p n t -> p g (n t)")
    q_rot = out_0.rearrange("b s h d -> (b s) h d")
    k_rot = out_1.rearrange("b s h d -> (b s) h d")
    v_out = out_2.rearrange("b s h d -> (b s) h d")

    with ExitStack() as ctx:
        ctx.enter_context(tc.manual_schedule())
        consts = ctx.enter_context(tc.tile_pool(name="consts", bufs=1))
        stage = ctx.enter_context(tc.tile_pool(name="stage", bufs=2))
        q_pieces = ctx.enter_context(tc.tile_pool(name="q_pieces", bufs=Q_PIECE_BUFS))
        kv_pieces = ctx.enter_context(tc.tile_pool(name="kv_pieces", bufs=KV_PIECE_BUFS))
        tail_pieces = ctx.enter_context(tc.tile_pool(name="tail_pieces", bufs=TAIL_PIECE_BUFS))
        kv_results = ctx.enter_context(tc.tile_pool(name="kv_results", bufs=KV_BANKS))
        psum_x = ctx.enter_context(tc.psum_pool(name="psum_x", bufs=2))
        psum_out = ctx.enter_context(tc.psum_pool(name="psum_out", bufs=1))

        x_sb = consts.tile([P, HIDDEN], BF16)
        nc.sync.dma_start(out=x_sb[:], in_=x)

        q_planes = consts.tile([P, PLANE_SETS, Q_COLS], U8, align_bytes=64)
        kv_planes = consts.tile([P, PLANE_SETS, KV_COLS], U8, align_bytes=64)
        nc.vector.memset(q_planes[:].bitcast(I32), 0)
        nc.vector.memset(kv_planes[:].bitcast(I32), 0)
        load_scale_planes(nc, q_planes, Wq_scales)
        load_scale_planes(nc, kv_planes, Wkv_scales)

        cos_t, sin_t = build_rotary_tables(nc, consts)
        identity = consts.tile([P, P], F32)
        make_identity(nc, identity[:])

        x_words = x_sb[:].bitcast(F32)
        x_codes = consts.tile([P, GROUPS, P], U32, align_bytes=64)
        x_scales = consts.tile([P, GROUPS, P], U8, align_bytes=64)
        for part in range(X_PARTS):
            grouped = stage.tile([P, PART_GROUPS, P, PACK], BF16, align_bytes=64)
            grouped_words = grouped[:].bitcast(F32)
            for pair in range(PART_GROUPS // 2):
                turned = psum_x.tile([P, 2, 2, P], F32)
                for i in range(2):
                    first = (part * PART_GROUPS + 2 * pair + i) * WORDS_PER_GROUP
                    for u in range(2):
                        nc.tensor.transpose(
                            out=turned[:, i, u, :],
                            in_=x_words[:, first + u : first + WORDS_PER_GROUP : 2],
                            identity=identity[:],
                        )
                copy = nc.vector.tensor_copy if pair == 0 else nc.scalar.copy
                copy(
                    out=grouped_words[:, 2 * pair : 2 * pair + 2, :, :],
                    in_=turned[:].rearrange("p i u r -> p i r u"),
                )
            part_groups = slice(part * PART_GROUPS, (part + 1) * PART_GROUPS)
            nc.vector.quantize_mx(
                out=x_codes[:, part_groups, :].rearrange("p g r -> p (g r)").bitcast(FP8X4),
                scales=x_scales[:, part_groups, :].rearrange("p g r -> p (g r)"),
                in_=grouped[:].rearrange("p g r t -> p (g r t)"),
            )

        def accumulate(pieces, words, planes, banks, first_col, groups):
            width = len(banks) * BANK_COLS
            for g in groups:
                piece = pieces.tile([P, width], U32, align_bytes=64)
                nc.sync.dma_start(
                    out=piece[:].bitcast(I32),
                    in_=words[:, g, PACK * first_col : PACK * (first_col + width)].bitcast(I32),
                )
                s, j = divmod(g, PLANES_PER_TILE)
                for b, bank in enumerate(banks):
                    nc.tensor.matmul_mx(
                        out=bank[:],
                        lhsT=x_codes[:, g, :].bitcast(FP8X4),
                        lhsT_scale=x_scales[:, g, :],
                        rhs=piece[:, b * BANK_COLS : (b + 1) * BANK_COLS].bitcast(FP8X4),
                        rhs_scale=planes[
                            SCALE_ROWS * j : P,
                            s,
                            first_col + b * BANK_COLS : first_col + (b + 1) * BANK_COLS,
                        ],
                        start=(g == 0),
                        stop=(g == GROUPS - 1),
                    )

        def rotate(rotated, crossed, heads):
            n = heads.shape[1]
            nc.vector.tensor_tensor(
                out=rotated,
                in0=heads,
                in1=cos_t[:].unsqueeze(1).to_broadcast([P, n, HEAD_DIM]),
                op=ALU.mult,
            )
            nc.vector.tensor_tensor(
                out=crossed.rearrange("p h (two d) -> p h two d", two=2),
                in0=heads.rearrange("p h (two d) -> p h two d", two=2)[:, :, ::-1, :],
                in1=sin_t[:]
                .rearrange("p (two d) -> p two d", two=2)
                .unsqueeze(1)
                .to_broadcast([P, n, 2, HALF]),
                op=ALU.mult,
            )
            nc.vector.tensor_tensor(out=rotated, in0=rotated, in1=crossed, op=ALU.add)

        q_banks = [psum_out.tile([P, BANK_COLS], F32, name="q_bank%d" % b) for b in range(Q_BANKS)]
        accumulate(q_pieces, q_words, q_planes, q_banks, 0, range(GROUPS))
        q_rotated = consts.tile([P, HEADS, HEAD_DIM], F32)
        q_crossed = consts.tile([P, HEADS, HEAD_DIM], F32)
        q_bank_heads = BANK_COLS // HEAD_DIM
        for b in range(Q_BANKS):
            these = slice(b * q_bank_heads, (b + 1) * q_bank_heads)
            rotate(
                q_rotated[:, these, :],
                q_crossed[:, these, :],
                q_banks[b][:].rearrange("p (h d) -> p h d", d=HEAD_DIM),
            )

        kv_banks = [psum_out.tile([P, BANK_COLS], F32, name="kv_bank%d" % b) for b in range(KV_BANKS)]
        whole = GROUPS - TAIL_GROUPS
        accumulate(kv_pieces, kv_words, kv_planes, kv_banks, 0, range(whole))
        stairs = [
            (whole + 2, 0, 3),
            (whole + 3, 0, 3),
            (whole + 1, 0, 2),
            (whole, 0, 1),
            (whole, 1, 3),
            (whole + 1, 2, 2),
            (whole + 2, 3, 1),
            (whole + 3, 3, 1),
        ]
        passes_done = [whole] * KV_BANKS
        for step, (g, first_bank, n_banks) in enumerate(stairs):
            piece = tail_pieces.tile([P, n_banks * BANK_COLS], U32, align_bytes=64, name="stair%d" % step)
            first_col = first_bank * BANK_COLS
            nc.sync.dma_start(
                out=piece[:].bitcast(I32),
                in_=kv_words[:, g, PACK * first_col : PACK * (first_col + n_banks * BANK_COLS)].bitcast(I32),
            )
            s, j = divmod(g, PLANES_PER_TILE)
            for i in range(n_banks):
                b = first_bank + i
                passes_done[b] += 1
                nc.tensor.matmul_mx(
                    out=kv_banks[b][:],
                    lhsT=x_codes[:, g, :].bitcast(FP8X4),
                    lhsT_scale=x_scales[:, g, :],
                    rhs=piece[:, i * BANK_COLS : (i + 1) * BANK_COLS].bitcast(FP8X4),
                    rhs_scale=kv_planes[SCALE_ROWS * j : P, s, b * BANK_COLS : (b + 1) * BANK_COLS],
                    start=False,
                    stop=(passes_done[b] == GROUPS),
                )

        nc.sync.dma_start(out=q_rot, in_=q_rotated[:])
        kv_bank_heads = BANK_COLS // (2 * HEAD_DIM)
        k_rotated = consts.tile([P, HEADS, HEAD_DIM], F32)
        values = consts.tile([P, HEADS, HEAD_DIM], F32)
        stored_after = {1: 0, 2: 2, 3: 3}
        for b in range(KV_BANKS):
            these = slice(b * kv_bank_heads, (b + 1) * kv_bank_heads)
            k_and_v = kv_banks[b][:].rearrange("p (h c d) -> p h c d", c=2, d=HEAD_DIM)
            k_crossed = kv_results.tile([P, kv_bank_heads, HEAD_DIM], F32)
            rotate(k_rotated[:, these, :], k_crossed[:], k_and_v[:, :, 0, :])
            nc.scalar.copy(out=values[:, these, :], in_=k_and_v[:, :, 1, :])
            if b in stored_after:
                ready = slice(stored_after[b] * kv_bank_heads, (b + 1) * kv_bank_heads)
                nc.sync.dma_start(out=v_out[:, ready, :], in_=values[:, ready, :])
                nc.sync.dma_start(out=k_rot[:, ready, :], in_=k_rotated[:, ready, :])
